import numpy as np
import ml_dtypes


def mxq(x, axis, fmt="e4m3"):
    dtype, down = {"e4m3": (ml_dtypes.float8_e4m3fn, 7), "e5m2": (ml_dtypes.float8_e5m2, 14)}[fmt]
    v = np.moveaxis(np.asarray(x, np.float32).astype(ml_dtypes.bfloat16).astype(np.float64), axis, -1)
    blocks = v.reshape(v.shape[:-1] + (-1, 32))
    amax = np.abs(blocks).max(-1, keepdims=True)
    byte = np.maximum(np.where(amax > 0, np.frexp(amax)[1] - 1 + 127, 0) - down, 1)
    scale = np.exp2(byte - 127.0)
    codes = (blocks / scale).astype(np.float32).astype(dtype).astype(np.float64)
    return np.moveaxis((codes * scale).reshape(v.shape), -1, axis)


WIDE = False


def mx_kscale(k):
    if not WIDE:
        return np.ones(k)
    levels = np.array([10, -10, 5, -5, 0])
    a = np.random.permutation(np.resize(levels, k // 512 * 4)).reshape(k // 512, 4)
    idx = np.arange(k)
    return np.exp2(a[idx // 512, idx % 128 // 32])


BF16 = ml_dtypes.bfloat16


def bf(x):
    return np.asarray(x, np.float32).astype(BF16)


def f64(x):
    return np.asarray(x).astype(np.float64)


B, X, N, OS = 2048, 512, 2304, 256
H = N - OS


def setup_inputs():
    s, t = mx_kscale(X), mx_kscale(H)
    std0 = np.sqrt(2.0 / X)
    std1 = np.sqrt(2.0 / (X + H))
    row_scale = np.concatenate([std0 * t, np.full(OS, std1)])
    bias_scale = np.concatenate([t, np.ones(OS)])
    return {"x": bf(np.random.standard_normal((B, X)) * s),
            "w0": bf(np.random.standard_normal((N, X)) * row_scale[:, None] / s),
            "w1": bf(np.random.standard_normal((OS, H)) * std1 / t),
            "biases": bf(np.random.random(N) * bias_scale)}


def reference(x, w0, w1, biases):
    n = w0.shape[0]
    os_ = w1.shape[0]
    z = (mxq(f64(x), 1, "e4m3") @ mxq(f64(w0), 1, "e4m3").T) + f64(biases)
    h = np.maximum(z[:, : n - os_], 0.0)
    return z[:, n - os_:] + (mxq(h, 1, "e4m3") @ mxq(f64(w1), 1, "e4m3").T)

@@ -1,0 +1,288 @@
+import concourse.mybir as mybir
+from concourse.masks import make_identity
+
+BF16 = mybir.dt.bfloat16
+F32 = mybir.dt.float32
+U32 = mybir.dt.uint32
+U8 = mybir.dt.uint8
+FP8X4 = mybir.dt.float8_e4m3fn_x4
+RELU = mybir.ActivationFunctionType.Relu
+ADD = mybir.AluOpType.add
+
+P = 128
+PACK = 4
+K_PASS = P * PACK
+HALF = 2
+
+BATCH = 2048
+X_DIM = 512
+HIDDEN = 2048
+OUT_NODES = 256
+
+CHUNK = 512
+CHUNKS = BATCH // CHUNK
+GROUPS = HIDDEN // K_PASS
+
+STEPS = CHUNKS * GROUPS
+LAG = 2
+PIECES = 2
+
+AHEAD = 3
+PER_STEP = 2
+VECTOR_EVERY = 3
+
+FLOPS = 2 * BATCH * X_DIM * (HIDDEN + OUT_NODES) + 2 * BATCH * HIDDEN * OUT_NODES
+
+
+def tile_spn_kernel(tc, x, w0, w1, biases, out):
+    nc = tc.nc
+    with (
+        tc.tile_pool(name="const", bufs=1) as const,
+        tc.tile_pool(name="rows", bufs=1) as rows_pool,
+        tc.tile_pool(name="quantised", bufs=1) as quantised,
+        tc.tile_pool(name="grouped", bufs=3) as grouped_pool,
+        tc.tile_pool(name="planes", bufs=3) as planes_pool,
+        tc.tile_pool(name="hidden", bufs=2) as hidden_pool,
+        tc.tile_pool(name="result", bufs=2) as result_pool,
+        tc.psum_pool(name="banks", bufs=4) as banks,
+        tc.psum_pool(name="sums", bufs=1) as sums,
+        tc.manual_schedule(),
+    ):
+        hidden_bias_bf = const.tile([P, GROUPS, PACK], BF16)
+        nc.scalar.dma_start(
+            out=hidden_bias_bf[:],
+            in_=biases[0:HIDDEN].rearrange("(g p t) -> p g t", p=P, t=PACK),
+        )
+        identity = const.tile([P, P], F32)
+        make_identity(nc, identity[:])
+        hidden_bias = const.tile([P, GROUPS * PACK], F32)
+        nc.gpsimd.tensor_copy(
+            out=hidden_bias[:], in_=hidden_bias_bf[:].rearrange("p g t -> p (g t)")
+        )
+
+        x_codes = quantised.tile([P, BATCH], U32, align_bytes=64)
+        x_scales = quantised.tile([P, BATCH], U8, align_bytes=64)
+        w0_codes = quantised.tile([P, HIDDEN], U32, align_bytes=64)
+        w0_scales = quantised.tile([P, HIDDEN], U8, align_bytes=64)
+        w0_out_codes = quantised.tile([P, OUT_NODES], U32, align_bytes=64)
+        w0_out_scales = quantised.tile([P, OUT_NODES], U8, align_bytes=64)
+        w1_codes = quantised.tile([P, GROUPS * OUT_NODES], U32, align_bytes=64)
+        w1_scales = quantised.tile([P, GROUPS * OUT_NODES], U8, align_bytes=64)
+
+        def halves_side_by_side(rows):
+            words = rows.bitcast(F32)
+            return [words[:, P * u : P * (u + 1)] for u in range(HALF)]
+
+        def halves_alternating(rows, g):
+            words = rows.bitcast(F32)
+            return [words[:, HALF * P * g + u : HALF * P * (g + 1) : HALF] for u in range(HALF)]
+
+        def block_of_512_rows(source, first, name, codes, scales):
+            rows = rows_pool.tile([P, PACK, X_DIM], BF16, name=name)
+            nc.sync.dma_start(
+                out=rows[:],
+                in_=source[first : first + K_PASS, :].rearrange("(p j) k -> p j k", j=PACK),
+            )
+            row_tiles = [halves_side_by_side(rows[:, j, :]) for j in range(PACK)]
+            columns = slice(first, first + K_PASS)
+            return row_tiles, codes[:, columns], scales[:, columns]
+
+        def x_chunk(c):
+            return block_of_512_rows(x, c * CHUNK, "x_rows%d" % c, x_codes, x_scales)
+
+        def w0_group(g):
+            return block_of_512_rows(w0, g * K_PASS, "w0_rows%d" % g, w0_codes, w0_scales)
+
+        operands = [x_chunk(0)] + [w0_group(g) for g in range(GROUPS - 1)]
+
+        w0_out_rows = rows_pool.tile([P, OUT_NODES // P, X_DIM], BF16)
+        nc.sync.dma_start(
+            out=w0_out_rows[:],
+            in_=w0[HIDDEN : HIDDEN + OUT_NODES, :].rearrange("(a p) k -> p a k", p=P),
+        )
+        operands.append(
+            (
+                [halves_side_by_side(w0_out_rows[:, a, :]) for a in range(OUT_NODES // P)],
+                w0_out_codes[:],
+                w0_out_scales[:],
+            )
+        )
+        w1_rows = rows_pool.tile([P, OUT_NODES // P, HIDDEN], BF16)
+        nc.sync.dma_start(out=w1_rows[:], in_=w1.rearrange("(a p) k -> p a k", p=P))
+
+        def w1_two_groups(first_g):
+            columns = slice(first_g * OUT_NODES, (first_g + 2) * OUT_NODES)
+            row_tiles = [
+                halves_alternating(w1_rows[:, a, :], g)
+                for g in range(first_g, first_g + 2)
+                for a in range(OUT_NODES // P)
+            ]
+            return row_tiles, w1_codes[:, columns], w1_scales[:, columns]
+
+        operands += [w1_two_groups(0), w0_group(GROUPS - 1), x_chunk(1), w1_two_groups(2)]
+        operands += [x_chunk(c) for c in range(2, CHUNKS)]
+
+        out_bias_bf = const.tile([P, OUT_NODES], BF16)
+        nc.sync.dma_start(
+            out=out_bias_bf[:], in_=biases[HIDDEN : HIDDEN + OUT_NODES].partition_broadcast(P)
+        )
+        out_bias = const.tile([P, OUT_NODES], F32)
+        nc.gpsimd.tensor_copy(out=out_bias[:], in_=out_bias_bf[:])
+
+        grouped_of = {}
+
+        def transpose_operand(i):
+            row_tiles = operands[i][0]
+            grouped = grouped_pool.tile(
+                [P, PACK * K_PASS], BF16, align_bytes=64, name="grouped"
+            )
+            grouped_of[i] = grouped
+            grouped_words = grouped[:].bitcast(F32)
+            for first in range(0, len(row_tiles), 2):
+                bank = banks.tile([P, CHUNK], F32, name="bank")
+                for r in range(2):
+                    for u in range(HALF):
+                        quarter = HALF * r + u
+                        nc.tensor.transpose(
+                            bank[:, P * quarter : P * (quarter + 1)],
+                            row_tiles[first + r][u],
+                            identity[:],
+                        )
+                bank_number = i * 2 + first // 2
+                if bank_number % VECTOR_EVERY == VECTOR_EVERY - 1:
+                    copy = nc.vector.tensor_copy
+                else:
+                    copy = nc.scalar.copy
+                copy(
+                    out=grouped_words[:, HALF * P * first : HALF * P * (first + 2)].rearrange(
+                        "p (r b u) -> p r b u", r=2, u=HALF
+                    ),
+                    in_=bank[:].rearrange("p (r u b) -> p r b u", r=2, u=HALF),
+                )
+
+        def quantise_operand(i):
+            row_tiles, codes, scales = operands[i]
+            nc.vector.quantize_mx(
+                out=codes.bitcast(FP8X4),
+                scales=scales,
+                in_=grouped_of[i][:, 0 : PACK * P * len(row_tiles)],
+            )
+
+        def prepare(i):
+            if i < len(operands):
+                transpose_operand(i)
+            if 0 < i <= len(operands):
+                quantise_operand(i - 1)
+
+        def first_stage(c, g):
+            planes = planes_pool.tile([P, PACK, CHUNK], BF16, name="planes")
+            for t in range(PACK):
+                nodes = slice(g * K_PASS + t * P, g * K_PASS + (t + 1) * P)
+                batch = slice(c * CHUNK, (c + 1) * CHUNK)
+                bank = banks.tile([P, CHUNK], F32, name="bank")
+                nc.tensor.matmul_mx(
+                    out=bank[:],
+                    lhsT=w0_codes[:, nodes].bitcast(FP8X4),
+                    lhsT_scale=w0_scales[:, nodes],
+                    rhs=x_codes[:, batch].bitcast(FP8X4),
+                    rhs_scale=x_scales[:, batch],
+                    start=True,
+                    stop=True,
+                )
+                nc.scalar.activation(
+                    out=planes[:, t, :],
+                    in_=bank[:],
+                    func=RELU,
+                    bias=hidden_bias[:, g * PACK + t : g * PACK + t + 1],
+                    scale=1.0,
+                )
+            return planes
+
+        def regroup_and_quantise(planes, codes, scales):
+            h_grouped = hidden_pool.tile([P, PACK * CHUNK], BF16, align_bytes=64, name="h_grouped")
+            width = CHUNK // PIECES
+            for piece in range(PIECES):
+                batch = slice(piece * width, (piece + 1) * width)
+                nc.vector.tensor_copy(
+                    out=h_grouped[:, PACK * piece * width : PACK * (piece + 1) * width].rearrange(
+                        "p (c i t) -> p c t i", i=4, t=PACK
+                    ),
+                    in_=planes[:, :, batch].rearrange("p t (c i) -> p c t i", i=4),
+                )
+            for piece in range(PIECES):
+                batch = slice(piece * width, (piece + 1) * width)
+                nc.vector.quantize_mx(
+                    out=codes[:, batch].bitcast(FP8X4),
+                    scales=scales[:, batch],
+                    in_=h_grouped[:, PACK * piece * width : PACK * (piece + 1) * width],
+                )
+
+        def second_stage(c, g, h_codes, h_scales, accs):
+            weights = slice(g * OUT_NODES, (g + 1) * OUT_NODES)
+            for j in range(PACK):
+                if g == 0:
+                    batch = slice(c * CHUNK + j * P, c * CHUNK + (j + 1) * P)
+                    nc.tensor.matmul_mx(
+                        out=accs[j][:],
+                        lhsT=x_codes[:, batch].bitcast(FP8X4),
+                        lhsT_scale=x_scales[:, batch],
+                        rhs=w0_out_codes[:].bitcast(FP8X4),
+                        rhs_scale=w0_out_scales[:],
+                        start=True,
+                        stop=False,
+                    )
+                batch = slice(g * CHUNK + j * P, g * CHUNK + (j + 1) * P)
+                nc.tensor.matmul_mx(
+                    out=accs[j][:],
+                    lhsT=h_codes[:, batch].bitcast(FP8X4),
+                    lhsT_scale=h_scales[:, batch],
+                    rhs=w1_codes[:, weights].bitcast(FP8X4),
+                    rhs_scale=w1_scales[:, weights],
+                    start=False,
+                    stop=(g == GROUPS - 1),
+                )
+
+        def finish(c, accs):
+            result = result_pool.tile([P, PACK, OUT_NODES], F32, name="result")
+            for j in range(PACK):
+                nc.vector.tensor_tensor(
+                    out=result[:, j, :], in0=accs[j][:], in1=out_bias[:], op=ADD
+                )
+            nc.sync.dma_start(
+                out=out[c * CHUNK : (c + 1) * CHUNK, :].rearrange("(p j) o -> p j o", j=PACK),
+                in_=result[:],
+            )
+
+        for i in range(AHEAD):
+            prepare(i)
+
+        h_codes_of = {}
+        h_scales_of = {}
+        accs_of = {}
+        for step in range(STEPS + LAG):
+            if step < STEPS:
+                c, g = divmod(step, GROUPS)
+                if g == 0:
+                    h_codes_of[c] = hidden_pool.tile(
+                        [P, GROUPS * CHUNK], U32, align_bytes=64, name="h_codes"
+                    )
+                    h_scales_of[c] = hidden_pool.tile(
+                        [P, GROUPS * CHUNK], U8, align_bytes=64, name="h_scales"
+                    )
+                planes = first_stage(c, g)
+            if step >= LAG:
+                late_c, late_g = divmod(step - LAG, GROUPS)
+                if late_g == 0:
+                    accs_of[late_c] = [
+                        sums.tile([P, OUT_NODES], F32, name="acc%d" % j) for j in range(PACK)
+                    ]
+                second_stage(
+                    late_c, late_g, h_codes_of[late_c], h_scales_of[late_c], accs_of[late_c]
+                )
+                if late_g == GROUPS - 1:
+                    finish(late_c, accs_of[late_c])
+            prepare(AHEAD + PER_STEP * step)
+            if step < STEPS:
+                columns = slice(g * CHUNK, (g + 1) * CHUNK)
+                regroup_and_quantise(planes, h_codes_of[c][:, columns], h_scales_of[c][:, columns])
+            prepare(AHEAD + PER_STEP * step + 1)

@@ -27,7 +27,7 @@ STEPS = CHUNKS * GROUPS
 LAG = 2
 PIECES = 2
 
-AHEAD = 3
+AT_ONCE = 2
 PER_STEP = 2
 VECTOR_EVERY = 3
 
@@ -43,7 +43,7 @@ def tile_spn_kernel(tc, x, w0, w1, biases, out):
         tc.tile_pool(name="grouped", bufs=3) as grouped_pool,
         tc.tile_pool(name="planes", bufs=3) as planes_pool,
         tc.tile_pool(name="hidden", bufs=2) as hidden_pool,
-        tc.tile_pool(name="result", bufs=2) as result_pool,
+        tc.tile_pool(name="result", bufs=4) as result_pool,
         tc.psum_pool(name="banks", bufs=4) as banks,
         tc.psum_pool(name="sums", bufs=1) as sums,
         tc.manual_schedule(),
@@ -78,12 +78,12 @@ def tile_spn_kernel(tc, x, w0, w1, biases, out):
             return [words[:, HALF * P * g + u : HALF * P * (g + 1) : HALF] for u in range(HALF)]
 
         def block_of_512_rows(source, first, name, codes, scales):
-            rows = rows_pool.tile([P, PACK, X_DIM], BF16, name=name)
-            nc.sync.dma_start(
-                out=rows[:],
-                in_=source[first : first + K_PASS, :].rearrange("(p j) k -> p j k", j=PACK),
-            )
-            row_tiles = [halves_side_by_side(rows[:, j, :]) for j in range(PACK)]
+            by_partition = source[first : first + K_PASS, :].rearrange("(p j) k -> p j k", j=PACK)
+            row_tiles = []
+            for j in range(0, PACK, 2):
+                rows = rows_pool.tile([P, 2, X_DIM], BF16, name="%s_%d" % (name, j))
+                nc.sync.dma_start(out=rows[:], in_=by_partition[:, j : j + 2, :])
+                row_tiles += [halves_side_by_side(rows[:, r, :]) for r in range(2)]
             columns = slice(first, first + K_PASS)
             return row_tiles, codes[:, columns], scales[:, columns]
 
@@ -149,7 +149,7 @@ def tile_spn_kernel(tc, x, w0, w1, biases, out):
                             identity[:],
                         )
                 bank_number = i * 2 + first // 2
-                if bank_number % VECTOR_EVERY == VECTOR_EVERY - 1:
+                if bank_number % VECTOR_EVERY == 0:
                     copy = nc.vector.tensor_copy
                 else:
                     copy = nc.scalar.copy
@@ -171,7 +171,7 @@ def tile_spn_kernel(tc, x, w0, w1, biases, out):
         def prepare(i):
             if i < len(operands):
                 transpose_operand(i)
-            if 0 < i <= len(operands):
+            if AT_ONCE < i <= len(operands):
                 quantise_operand(i - 1)
 
         def first_stage(c, g):
@@ -243,18 +243,16 @@ def tile_spn_kernel(tc, x, w0, w1, biases, out):
                 )
 
         def finish(c, accs):
-            result = result_pool.tile([P, PACK, OUT_NODES], F32, name="result")
+            rows_of_out = out[c * CHUNK : (c + 1) * CHUNK, :].rearrange("(p j) o -> p j o", j=PACK)
             for j in range(PACK):
-                nc.vector.tensor_tensor(
-                    out=result[:, j, :], in0=accs[j][:], in1=out_bias[:], op=ADD
-                )
-            nc.sync.dma_start(
-                out=out[c * CHUNK : (c + 1) * CHUNK, :].rearrange("(p j) o -> p j o", j=PACK),
-                in_=result[:],
-            )
+                result = result_pool.tile([P, OUT_NODES], F32, name="result")
+                nc.vector.tensor_tensor(out=result[:], in0=accs[j][:], in1=out_bias[:], op=ADD)
+                nc.sync.dma_start(out=rows_of_out[:, j, :], in_=result[:])
 
-        for i in range(AHEAD):
-            prepare(i)
+        for i in range(AT_ONCE):
+            transpose_operand(i)
+            quantise_operand(i)
+        prepare(AT_ONCE)
 
         h_codes_of = {}
         h_scales_of = {}
@@ -281,8 +279,8 @@ def tile_spn_kernel(tc, x, w0, w1, biases, out):
                 )
                 if late_g == GROUPS - 1:
                     finish(late_c, accs_of[late_c])
-            prepare(AHEAD + PER_STEP * step)
+            for i in range(PER_STEP):
+                prepare(AT_ONCE + 1 + PER_STEP * step + i)
             if step < STEPS:
                 columns = slice(g * CHUNK, (g + 1) * CHUNK)
                 regroup_and_quantise(planes, h_codes_of[c][:, columns], h_scales_of[c][:, columns])
-            prepare(AHEAD + PER_STEP * step + 1)

@@ -8,6 +8,7 @@ U8 = mybir.dt.uint8
 FP8X4 = mybir.dt.float8_e4m3fn_x4
 RELU = mybir.ActivationFunctionType.Relu
 ADD = mybir.AluOpType.add
+MAX = mybir.AluOpType.max
 
 P = 128
 PACK = 4
@@ -30,6 +31,7 @@ PIECES = 2
 AT_ONCE = 2
 PER_STEP = 2
 VECTOR_EVERY = 3
+VECTOR_RELU_EVERY = 16
 
 FLOPS = 2 * BATCH * X_DIM * (HIDDEN + OUT_NODES) + 2 * BATCH * HIDDEN * OUT_NODES
 
@@ -189,13 +191,16 @@ def tile_spn_kernel(tc, x, w0, w1, biases, out):
                     start=True,
                     stop=True,
                 )
-                nc.scalar.activation(
-                    out=planes[:, t, :],
-                    in_=bank[:],
-                    func=RELU,
-                    bias=hidden_bias[:, g * PACK + t : g * PACK + t + 1],
-                    scale=1.0,
-                )
+                bias = hidden_bias[:, g * PACK + t : g * PACK + t + 1]
+                bank_number = (c * GROUPS + g) * PACK + t
+                if bank_number % VECTOR_RELU_EVERY == VECTOR_RELU_EVERY - 1:
+                    nc.vector.tensor_scalar(
+                        out=planes[:, t, :], in0=bank[:], scalar1=bias, scalar2=0.0, op0=ADD, op1=MAX
+                    )
+                else:
+                    nc.scalar.activation(
+                        out=planes[:, t, :], in_=bank[:], func=RELU, bias=bias, scale=1.0
+                    )
             return planes
 
         def regroup_and_quantise(planes, codes, scales):

@@ -8,7 +8,6 @@ U8 = mybir.dt.uint8
 FP8X4 = mybir.dt.float8_e4m3fn_x4
 RELU = mybir.ActivationFunctionType.Relu
 ADD = mybir.AluOpType.add
-MAX = mybir.AluOpType.max
 
 P = 128
 PACK = 4
@@ -31,7 +30,6 @@ PIECES = 2
 AT_ONCE = 2
 PER_STEP = 2
 VECTOR_EVERY = 3
-VECTOR_RELU_EVERY = 16
 
 FLOPS = 2 * BATCH * X_DIM * (HIDDEN + OUT_NODES) + 2 * BATCH * HIDDEN * OUT_NODES
 
@@ -50,17 +48,16 @@ def tile_spn_kernel(tc, x, w0, w1, biases, out):
         tc.psum_pool(name="sums", bufs=1) as sums,
         tc.manual_schedule(),
     ):
-        hidden_bias_bf = const.tile([P, GROUPS, PACK], BF16)
+        hidden_bias = const.tile([P, GROUPS, PACK], BF16)
         nc.scalar.dma_start(
-            out=hidden_bias_bf[:],
+            out=hidden_bias[:],
             in_=biases[0:HIDDEN].rearrange("(g p t) -> p g t", p=P, t=PACK),
         )
         identity = const.tile([P, P], F32)
         make_identity(nc, identity[:])
-        hidden_bias = const.tile([P, GROUPS * PACK], F32)
-        nc.gpsimd.tensor_copy(
-            out=hidden_bias[:], in_=hidden_bias_bf[:].rearrange("p g t -> p (g t)")
-        )
+        warm_up = const.tile([P, 1], F32)
+        nc.vector.memset(warm_up[:], 0.0)
+        nc.scalar.activation(out=warm_up[:], in_=warm_up[:], func=RELU)
 
         x_codes = quantised.tile([P, BATCH], U32, align_bytes=64)
         x_scales = quantised.tile([P, BATCH], U8, align_bytes=64)
@@ -191,16 +188,13 @@ def tile_spn_kernel(tc, x, w0, w1, biases, out):
                     start=True,
                     stop=True,
                 )
-                bias = hidden_bias[:, g * PACK + t : g * PACK + t + 1]
-                bank_number = (c * GROUPS + g) * PACK + t
-                if bank_number % VECTOR_RELU_EVERY == VECTOR_RELU_EVERY - 1:
-                    nc.vector.tensor_scalar(
-                        out=planes[:, t, :], in0=bank[:], scalar1=bias, scalar2=0.0, op0=ADD, op1=MAX
-                    )
-                else:
-                    nc.scalar.activation(
-                        out=planes[:, t, :], in_=bank[:], func=RELU, bias=bias, scale=1.0
-                    )
+                nc.scalar.activation(
+                    out=planes[:, t, :],
+                    in_=bank[:],
+                    func=RELU,
+                    bias=hidden_bias[:, g, t : t + 1],
+                    scale=1.0,
+                )
             return planes
 
         def regroup_and_quantise(planes, codes, scales):

import concourse.mybir as mybir
from concourse.masks import make_identity

BF16 = mybir.dt.bfloat16
F32 = mybir.dt.float32
U32 = mybir.dt.uint32
U8 = mybir.dt.uint8
FP8X4 = mybir.dt.float8_e4m3fn_x4
RELU = mybir.ActivationFunctionType.Relu
ADD = mybir.AluOpType.add

P = 128
PACK = 4
K_PASS = P * PACK
HALF = 2

BATCH = 2048
X_DIM = 512
HIDDEN = 2048
OUT_NODES = 256

CHUNK = 512
CHUNKS = BATCH // CHUNK
GROUPS = HIDDEN // K_PASS

STEPS = CHUNKS * GROUPS
LAG = 2
PIECES = 2

AT_ONCE = 2
PER_STEP = 2
VECTOR_EVERY = 3

FLOPS = 2 * BATCH * X_DIM * (HIDDEN + OUT_NODES) + 2 * BATCH * HIDDEN * OUT_NODES


def tile_spn_kernel(tc, x, w0, w1, biases, out):
    nc = tc.nc
    with (
        tc.tile_pool(name="const", bufs=1) as const,
        tc.tile_pool(name="rows", bufs=1) as rows_pool,
        tc.tile_pool(name="quantised", bufs=1) as quantised,
        tc.tile_pool(name="grouped", bufs=3) as grouped_pool,
        tc.tile_pool(name="planes", bufs=3) as planes_pool,
        tc.tile_pool(name="hidden", bufs=2) as hidden_pool,
        tc.tile_pool(name="result", bufs=4) as result_pool,
        tc.psum_pool(name="banks", bufs=4) as banks,
        tc.psum_pool(name="sums", bufs=1) as sums,
        tc.manual_schedule(),
    ):
        hidden_bias = const.tile([P, GROUPS, PACK], BF16)
        nc.scalar.dma_start(
            out=hidden_bias[:],
            in_=biases[0:HIDDEN].rearrange("(g p t) -> p g t", p=P, t=PACK),
        )
        identity = const.tile([P, P], F32)
        make_identity(nc, identity[:])
        warm_up = const.tile([P, 1], F32)
        nc.vector.memset(warm_up[:], 0.0)
        nc.scalar.activation(out=warm_up[:], in_=warm_up[:], func=RELU)

        x_codes = quantised.tile([P, BATCH], U32, align_bytes=64)
        x_scales = quantised.tile([P, BATCH], U8, align_bytes=64)
        w0_codes = quantised.tile([P, HIDDEN], U32, align_bytes=64)
        w0_scales = quantised.tile([P, HIDDEN], U8, align_bytes=64)
        w0_out_codes = quantised.tile([P, OUT_NODES], U32, align_bytes=64)
        w0_out_scales = quantised.tile([P, OUT_NODES], U8, align_bytes=64)
        w1_codes = quantised.tile([P, GROUPS * OUT_NODES], U32, align_bytes=64)
        w1_scales = quantised.tile([P, GROUPS * OUT_NODES], U8, align_bytes=64)

        def halves_side_by_side(rows):
            words = rows.bitcast(F32)
            return [words[:, P * u : P * (u + 1)] for u in range(HALF)]

        def halves_alternating(rows, g):
            words = rows.bitcast(F32)
            return [words[:, HALF * P * g + u : HALF * P * (g + 1) : HALF] for u in range(HALF)]

        def block_of_512_rows(source, first, name, codes, scales):
            by_partition = source[first : first + K_PASS, :].rearrange("(p j) k -> p j k", j=PACK)
            row_tiles = []
            for j in range(0, PACK, 2):
                rows = rows_pool.tile([P, 2, X_DIM], BF16, name="%s_%d" % (name, j))
                nc.sync.dma_start(out=rows[:], in_=by_partition[:, j : j + 2, :])
                row_tiles += [halves_side_by_side(rows[:, r, :]) for r in range(2)]
            columns = slice(first, first + K_PASS)
            return row_tiles, codes[:, columns], scales[:, columns]

        def x_chunk(c):
            return block_of_512_rows(x, c * CHUNK, "x_rows%d" % c, x_codes, x_scales)

        def w0_group(g):
            return block_of_512_rows(w0, g * K_PASS, "w0_rows%d" % g, w0_codes, w0_scales)

        operands = [x_chunk(0)] + [w0_group(g) for g in range(GROUPS - 1)]

        w0_out_rows = rows_pool.tile([P, OUT_NODES // P, X_DIM], BF16)
        nc.sync.dma_start(
            out=w0_out_rows[:],
            in_=w0[HIDDEN : HIDDEN + OUT_NODES, :].rearrange("(a p) k -> p a k", p=P),
        )
        operands.append(
            (
                [halves_side_by_side(w0_out_rows[:, a, :]) for a in range(OUT_NODES // P)],
                w0_out_codes[:],
                w0_out_scales[:],
            )
        )
        w1_rows = rows_pool.tile([P, OUT_NODES // P, HIDDEN], BF16)
        nc.sync.dma_start(out=w1_rows[:], in_=w1.rearrange("(a p) k -> p a k", p=P))

        def w1_two_groups(first_g):
            columns = slice(first_g * OUT_NODES, (first_g + 2) * OUT_NODES)
            row_tiles = [
                halves_alternating(w1_rows[:, a, :], g)
                for g in range(first_g, first_g + 2)
                for a in range(OUT_NODES // P)
            ]
            return row_tiles, w1_codes[:, columns], w1_scales[:, columns]

        operands += [w1_two_groups(0), w0_group(GROUPS - 1), x_chunk(1), w1_two_groups(2)]
        operands += [x_chunk(c) for c in range(2, CHUNKS)]

        out_bias_bf = const.tile([P, OUT_NODES], BF16)
        nc.sync.dma_start(
            out=out_bias_bf[:], in_=biases[HIDDEN : HIDDEN + OUT_NODES].partition_broadcast(P)
        )
        out_bias = const.tile([P, OUT_NODES], F32)
        nc.gpsimd.tensor_copy(out=out_bias[:], in_=out_bias_bf[:])

        grouped_of = {}

        def transpose_operand(i):
            row_tiles = operands[i][0]
            grouped = grouped_pool.tile(
                [P, PACK * K_PASS], BF16, align_bytes=64, name="grouped"
            )
            grouped_of[i] = grouped
            grouped_words = grouped[:].bitcast(F32)
            for first in range(0, len(row_tiles), 2):
                bank = banks.tile([P, CHUNK], F32, name="bank")
                for r in range(2):
                    for u in range(HALF):
                        quarter = HALF * r + u
                        nc.tensor.transpose(
                            bank[:, P * quarter : P * (quarter + 1)],
                            row_tiles[first + r][u],
                            identity[:],
                        )
                bank_number = i * 2 + first // 2
                if bank_number % VECTOR_EVERY == 0:
                    copy = nc.vector.tensor_copy
                else:
                    copy = nc.scalar.copy
                copy(
                    out=grouped_words[:, HALF * P * first : HALF * P * (first + 2)].rearrange(
                        "p (r b u) -> p r b u", r=2, u=HALF
                    ),
                    in_=bank[:].rearrange("p (r u b) -> p r b u", r=2, u=HALF),
                )

        def quantise_operand(i):
            row_tiles, codes, scales = operands[i]
            nc.vector.quantize_mx(
                out=codes.bitcast(FP8X4),
                scales=scales,
                in_=grouped_of[i][:, 0 : PACK * P * len(row_tiles)],
            )

        def prepare(i):
            if i < len(operands):
                transpose_operand(i)
            if AT_ONCE < i <= len(operands):
                quantise_operand(i - 1)

        def first_stage(c, g):
            planes = planes_pool.tile([P, PACK, CHUNK], BF16, name="planes")
            for t in range(PACK):
                nodes = slice(g * K_PASS + t * P, g * K_PASS + (t + 1) * P)
                batch = slice(c * CHUNK, (c + 1) * CHUNK)
                bank = banks.tile([P, CHUNK], F32, name="bank")
                nc.tensor.matmul_mx(
                    out=bank[:],
                    lhsT=w0_codes[:, nodes].bitcast(FP8X4),
                    lhsT_scale=w0_scales[:, nodes],
                    rhs=x_codes[:, batch].bitcast(FP8X4),
                    rhs_scale=x_scales[:, batch],
                    start=True,
                    stop=True,
                )
                nc.scalar.activation(
                    out=planes[:, t, :],
                    in_=bank[:],
                    func=RELU,
                    bias=hidden_bias[:, g, t : t + 1],
                    scale=1.0,
                )
            return planes

        def regroup_and_quantise(planes, codes, scales):
            h_grouped = hidden_pool.tile([P, PACK * CHUNK], BF16, align_bytes=64, name="h_grouped")
            width = CHUNK // PIECES
            for piece in range(PIECES):
                batch = slice(piece * width, (piece + 1) * width)
                nc.vector.tensor_copy(
                    out=h_grouped[:, PACK * piece * width : PACK * (piece + 1) * width].rearrange(
                        "p (c i t) -> p c t i", i=4, t=PACK
                    ),
                    in_=planes[:, :, batch].rearrange("p t (c i) -> p c t i", i=4),
                )
            for piece in range(PIECES):
                batch = slice(piece * width, (piece + 1) * width)
                nc.vector.quantize_mx(
                    out=codes[:, batch].bitcast(FP8X4),
                    scales=scales[:, batch],
                    in_=h_grouped[:, PACK * piece * width : PACK * (piece + 1) * width],
                )

        def second_stage(c, g, h_codes, h_scales, accs):
            weights = slice(g * OUT_NODES, (g + 1) * OUT_NODES)
            for j in range(PACK):
                if g == 0:
                    batch = slice(c * CHUNK + j * P, c * CHUNK + (j + 1) * P)
                    nc.tensor.matmul_mx(
                        out=accs[j][:],
                        lhsT=x_codes[:, batch].bitcast(FP8X4),
                        lhsT_scale=x_scales[:, batch],
                        rhs=w0_out_codes[:].bitcast(FP8X4),
                        rhs_scale=w0_out_scales[:],
                        start=True,
                        stop=False,
                    )
                batch = slice(g * CHUNK + j * P, g * CHUNK + (j + 1) * P)
                nc.tensor.matmul_mx(
                    out=accs[j][:],
                    lhsT=h_codes[:, batch].bitcast(FP8X4),
                    lhsT_scale=h_scales[:, batch],
                    rhs=w1_codes[:, weights].bitcast(FP8X4),
                    rhs_scale=w1_scales[:, weights],
                    start=False,
                    stop=(g == GROUPS - 1),
                )

        def finish(c, accs):
            rows_of_out = out[c * CHUNK : (c + 1) * CHUNK, :].rearrange("(p j) o -> p j o", j=PACK)
            for j in range(PACK):
                result = result_pool.tile([P, OUT_NODES], F32, name="result")
                nc.vector.tensor_tensor(out=result[:], in0=accs[j][:], in1=out_bias[:], op=ADD)
                nc.sync.dma_start(out=rows_of_out[:, j, :], in_=result[:])

        for i in range(AT_ONCE):
            transpose_operand(i)
            quantise_operand(i)
        prepare(AT_ONCE)

        h_codes_of = {}
        h_scales_of = {}
        accs_of = {}
        for step in range(STEPS + LAG):
            if step < STEPS:
                c, g = divmod(step, GROUPS)
                if g == 0:
                    h_codes_of[c] = hidden_pool.tile(
                        [P, GROUPS * CHUNK], U32, align_bytes=64, name="h_codes"
                    )
                    h_scales_of[c] = hidden_pool.tile(
                        [P, GROUPS * CHUNK], U8, align_bytes=64, name="h_scales"
                    )
                planes = first_stage(c, g)
            if step >= LAG:
                late_c, late_g = divmod(step - LAG, GROUPS)
                if late_g == 0:
                    accs_of[late_c] = [
                        sums.tile([P, OUT_NODES], F32, name="acc%d" % j) for j in range(PACK)
                    ]
                second_stage(
                    late_c, late_g, h_codes_of[late_c], h_scales_of[late_c], accs_of[late_c]
                )
                if late_g == GROUPS - 1:
                    finish(late_c, accs_of[late_c])
            for i in range(PER_STEP):
                prepare(AT_ONCE + 1 + PER_STEP * step + i)
            if step < STEPS:
                columns = slice(g * CHUNK, (g + 1) * CHUNK)
                regroup_and_quantise(planes, h_codes_of[c][:, columns], h_scales_of[c][:, columns])
